import numpy as np
import ml_dtypes


def mxq(x, axis, fmt="e4m3"):
    dtype, down = {"e4m3": (ml_dtypes.float8_e4m3fn, 7), "e5m2": (ml_dtypes.float8_e5m2, 14)}[fmt]
    v = np.moveaxis(np.asarray(x, np.float32).astype(ml_dtypes.bfloat16).astype(np.float64), axis, -1)
    blocks = v.reshape(v.shape[:-1] + (-1, 32))
    amax = np.abs(blocks).max(-1, keepdims=True)
    byte = np.maximum(np.where(amax > 0, np.frexp(amax)[1] - 1 + 127, 0) - down, 1)
    scale = np.exp2(byte - 127.0)
    codes = (blocks / scale).astype(np.float32).astype(dtype).astype(np.float64)
    return np.moveaxis((codes * scale).reshape(v.shape), -1, axis)


WIDE = False


def mx_kscale(k):
    if not WIDE:
        return np.ones(k)
    levels = np.array([10, -10, 5, -5, 0])
    a = np.random.permutation(np.resize(levels, k // 512 * 4)).reshape(k // 512, 4)
    idx = np.arange(k)
    return np.exp2(a[idx // 512, idx % 128 // 32])


BF16 = ml_dtypes.bfloat16


def bf(x):
    return np.asarray(x, np.float32).astype(BF16)


def f64(x):
    return np.asarray(x).astype(np.float64)


N, K, C = 1024, 256, 512


def draw(rows, f, total):
    x = np.random.standard_normal((rows, f.size))
    for v in np.unique(f):
        m = f == v
        x[:, m] -= x[:, m].mean(1, keepdims=True)
    top = (f == f.max()).astype(np.float64)
    return np.sqrt(K / (2.0 * np.sqrt(C))) * x * f + total * np.random.standard_normal((rows, 1)) * top / top.sum()


def setup_inputs():
    s = mx_kscale(C)
    return {"output": bf(draw(N, s, 0.3 * K)), "code_book": bf(draw(K, 1.0 / s, 0.3 * K))}


def reference(output, code_book):
    output, code_book = f64(output), f64(code_book)
    K, C = code_book.shape
    dot = mxq(output, 1, "e4m3") @ mxq(code_book, 1, "e4m3").T
    o_sum = np.sum(output, axis=1, keepdims=True)
    c_sum = np.sum(code_book, axis=1)[None, :]
    return (2.0 * dot + float(C) - o_sum - c_sum) / float(K)

@@ -1,0 +1,155 @@
+from contextlib import ExitStack
+
+import concourse.mybir as mybir
+from concourse.masks import make_identity
+
+F32 = mybir.dt.float32
+BF16 = mybir.dt.bfloat16
+U32 = mybir.dt.uint32
+U8 = mybir.dt.uint8
+FP8X4 = mybir.dt.float8_e4m3fn_x4
+ALU = mybir.AluOpType
+FUNC = mybir.ActivationFunctionType
+
+P = 128
+ROWS = 1024
+CODES = 256
+LENGTH = 512
+WORDS = LENGTH // 2
+ROW_TILES = ROWS // P
+CODE_TILES = CODES // P
+PAIR = 2
+CHUNKS = ROW_TILES // PAIR
+
+FLOPS = 2 * ROWS * CODES * LENGTH
+
+
+def sum_rows(nc, rows, scratch, total):
+    nc.vector.tensor_scalar(
+        out=scratch,
+        in0=rows,
+        scalar1=-1.0 / CODES,
+        scalar2=None,
+        op0=ALU.mult,
+        op1=ALU.add,
+        accum_out=total,
+    )
+
+
+def transpose_pair(nc, bank, rows, identity):
+    words = rows.bitcast(F32)
+    for j in range(PAIR):
+        for u in range(2):
+            nc.tensor.transpose(bank[:, j, u, :], words[:, j, u * P : (u + 1) * P], identity)
+
+
+def quantise_pair(nc, bank, grouped, codes, scales):
+    nc.scalar.copy(
+        out=grouped.bitcast(F32).rearrange("p (j n u) -> p j n u", j=PAIR, u=2),
+        in_=bank.rearrange("p j u n -> p j n u"),
+    )
+    nc.vector.quantize_mx(out=codes.bitcast(FP8X4), scales=scales, in_=grouped)
+
+
+def tile_codingclassifier_s_kernel(tc, output, code_book, out):
+    nc = tc.nc
+    x_view = output.rearrange("(p r) c -> p r c", r=ROW_TILES)
+    out_view = out.rearrange("(p r) k -> p r k", r=ROW_TILES)
+
+    with ExitStack() as ctx:
+        keep = ctx.enter_context(tc.tile_pool(name="keep", bufs=1))
+        x_pool = ctx.enter_context(tc.tile_pool(name="x_pool", bufs=CHUNKS))
+        work = ctx.enter_context(tc.tile_pool(name="work", bufs=3))
+        t_psum = ctx.enter_context(tc.psum_pool(name="t_psum", bufs=3))
+        dot_psum = ctx.enter_context(tc.psum_pool(name="dot_psum", bufs=3))
+        c_psum = ctx.enter_context(tc.psum_pool(name="c_psum", bufs=1))
+
+        y_rows = keep.tile([P, CODE_TILES, LENGTH], BF16)
+        nc.sync.dma_start(out=y_rows[:], in_=code_book.rearrange("(a p) c -> p a c", p=P))
+        x_chunks = []
+        for chunk in range(CHUNKS):
+            x_rows = x_pool.tile([P, PAIR, LENGTH], BF16)
+            nc.sync.dma_start(out=x_rows[:], in_=x_view[:, chunk * PAIR : (chunk + 1) * PAIR, :])
+            x_chunks.append(x_rows)
+
+        identity = keep.tile([P, P], F32)
+        make_identity(nc, identity[:])
+
+        warm = keep.tile([P, 1], F32)
+        nc.vector.memset(warm[:], 0.0)
+        warmed = keep.tile([P, 1], F32)
+        nc.scalar.activation(out=warmed[:], in_=warm[:], func=FUNC.Identity)
+
+        scratch = keep.tile([P, CODE_TILES + ROW_TILES, LENGTH], BF16)
+
+        c_part = keep.tile([P, CODE_TILES], F32)
+        for a in range(CODE_TILES):
+            sum_rows(nc, y_rows[:, a, :], scratch[:, a, :], c_part[:, a : a + 1])
+
+        y_bank = t_psum.tile([P, PAIR, 2, P], F32, tag="bank")
+        transpose_pair(nc, y_bank, y_rows[:], identity[:])
+        y_grouped = keep.tile([P, CODES * 4], BF16, align_bytes=64)
+        y_codes = keep.tile([P, CODES], U32, align_bytes=64)
+        y_scales = keep.tile([P, CODES], U8, align_bytes=64)
+        quantise_pair(nc, y_bank, y_grouped[:], y_codes[:], y_scales[:])
+
+        spread = c_psum.tile([P, CODES], F32)
+        for a in range(CODE_TILES):
+            nc.tensor.matmul(
+                out=spread[:, a * P : (a + 1) * P],
+                lhsT=c_part[:, a : a + 1].to_broadcast([P, P]),
+                rhs=identity[:],
+                start=True,
+                stop=True,
+            )
+        c_term = keep.tile([P, CODES], F32)
+        nc.scalar.activation(out=c_term[:], in_=spread[:], func=FUNC.Identity, bias=2.0, scale=1.0)
+
+        o_term = keep.tile([P, ROW_TILES], F32)
+        for chunk in range(CHUNKS):
+            x_rows = x_chunks[chunk]
+            for j in range(PAIR):
+                r = chunk * PAIR + j
+                sum_rows(nc, x_rows[:, j, :], scratch[:, CODE_TILES + r, :], o_term[:, r : r + 1])
+
+            x_bank = t_psum.tile([P, PAIR, 2, P], F32, tag="bank")
+            transpose_pair(nc, x_bank, x_rows[:], identity[:])
+            x_grouped = work.tile([P, PAIR * P * 4], BF16, align_bytes=64)
+            x_codes = work.tile([P, PAIR * P], U32, align_bytes=64)
+            x_scales = work.tile([P, PAIR * P], U8, align_bytes=64)
+            quantise_pair(nc, x_bank, x_grouped[:], x_codes[:], x_scales[:])
+
+            both_terms = work.tile([P, PAIR * CODES], F32)
+            dot = dot_psum.tile([P, PAIR * CODES], F32)
+            for j in range(PAIR):
+                r = chunk * PAIR + j
+                nc.scalar.activation(
+                    out=both_terms[:, j * CODES : (j + 1) * CODES],
+                    in_=c_term[:],
+                    func=FUNC.Identity,
+                    bias=o_term[:, r : r + 1],
+                    scale=1.0,
+                )
+                nc.tensor.matmul_mx(
+                    out=dot[:, j * CODES : (j + 1) * CODES],
+                    lhsT=x_codes[:, j * P : (j + 1) * P].bitcast(FP8X4),
+                    lhsT_scale=x_scales[:, j * P : (j + 1) * P],
+                    rhs=y_codes[:].bitcast(FP8X4),
+                    rhs_scale=y_scales[:],
+                    start=True,
+                    stop=True,
+                )
+
+            result = work.tile([P, PAIR * CODES], F32)
+            nc.vector.scalar_tensor_tensor(
+                out=result[:],
+                in0=dot[:],
+                scalar=2.0 / CODES,
+                in1=both_terms[:],
+                op0=ALU.mult,
+                op1=ALU.add,
+            )
+            nc.sync.dma_start(
+                out=out_view[:, chunk * PAIR : (chunk + 1) * PAIR, :],
+                in_=result[:].rearrange("p (j k) -> p j k", j=PAIR),
+            )

@@ -24,7 +24,7 @@ CHUNKS = ROW_TILES // PAIR
 FLOPS = 2 * ROWS * CODES * LENGTH
 
 
-def sum_rows(nc, rows, scratch, total):
+def sum_rows_vector(nc, rows, scratch, total):
     nc.vector.tensor_scalar(
         out=scratch,
         in0=rows,
@@ -36,19 +36,8 @@ def sum_rows(nc, rows, scratch, total):
     )
 
 
-def transpose_pair(nc, bank, rows, identity):
-    words = rows.bitcast(F32)
-    for j in range(PAIR):
-        for u in range(2):
-            nc.tensor.transpose(bank[:, j, u, :], words[:, j, u * P : (u + 1) * P], identity)
-
-
-def quantise_pair(nc, bank, grouped, codes, scales):
-    nc.scalar.copy(
-        out=grouped.bitcast(F32).rearrange("p (j n u) -> p j n u", j=PAIR, u=2),
-        in_=bank.rearrange("p j u n -> p j n u"),
-    )
-    nc.vector.quantize_mx(out=codes.bitcast(FP8X4), scales=scales, in_=grouped)
+def sum_rows_scalar(nc, rows, scratch, total):
+    nc.scalar.activation(out=scratch, in_=rows, func=FUNC.Identity, scale=-1.0 / CODES, accum_out=total)
 
 
 def tile_codingclassifier_s_kernel(tc, output, code_book, out):
@@ -57,20 +46,20 @@ def tile_codingclassifier_s_kernel(tc, output, code_book, out):
     out_view = out.rearrange("(p r) k -> p r k", r=ROW_TILES)
 
     with ExitStack() as ctx:
+        ctx.enter_context(tc.manual_schedule())
         keep = ctx.enter_context(tc.tile_pool(name="keep", bufs=1))
-        x_pool = ctx.enter_context(tc.tile_pool(name="x_pool", bufs=CHUNKS))
-        work = ctx.enter_context(tc.tile_pool(name="work", bufs=3))
-        t_psum = ctx.enter_context(tc.psum_pool(name="t_psum", bufs=3))
+        work = ctx.enter_context(tc.tile_pool(name="work", bufs=CHUNKS))
+        t_psum = ctx.enter_context(tc.psum_pool(name="t_psum", bufs=4))
         dot_psum = ctx.enter_context(tc.psum_pool(name="dot_psum", bufs=3))
         c_psum = ctx.enter_context(tc.psum_pool(name="c_psum", bufs=1))
 
-        y_rows = keep.tile([P, CODE_TILES, LENGTH], BF16)
+        y_rows = keep.tile([P, PAIR, LENGTH], BF16)
         nc.sync.dma_start(out=y_rows[:], in_=code_book.rearrange("(a p) c -> p a c", p=P))
-        x_chunks = []
+        pairs = [y_rows]
         for chunk in range(CHUNKS):
-            x_rows = x_pool.tile([P, PAIR, LENGTH], BF16)
+            x_rows = work.tile([P, PAIR, LENGTH], BF16)
             nc.sync.dma_start(out=x_rows[:], in_=x_view[:, chunk * PAIR : (chunk + 1) * PAIR, :])
-            x_chunks.append(x_rows)
+            pairs.append(x_rows)
 
         identity = keep.tile([P, P], F32)
         make_identity(nc, identity[:])
@@ -80,72 +69,86 @@ def tile_codingclassifier_s_kernel(tc, output, code_book, out):
         warmed = keep.tile([P, 1], F32)
         nc.scalar.activation(out=warmed[:], in_=warm[:], func=FUNC.Identity)
 
-        scratch = keep.tile([P, CODE_TILES + ROW_TILES, LENGTH], BF16)
-
-        c_part = keep.tile([P, CODE_TILES], F32)
-        for a in range(CODE_TILES):
-            sum_rows(nc, y_rows[:, a, :], scratch[:, a, :], c_part[:, a : a + 1])
-
-        y_bank = t_psum.tile([P, PAIR, 2, P], F32, tag="bank")
-        transpose_pair(nc, y_bank, y_rows[:], identity[:])
-        y_grouped = keep.tile([P, CODES * 4], BF16, align_bytes=64)
-        y_codes = keep.tile([P, CODES], U32, align_bytes=64)
-        y_scales = keep.tile([P, CODES], U8, align_bytes=64)
-        quantise_pair(nc, y_bank, y_grouped[:], y_codes[:], y_scales[:])
-
-        spread = c_psum.tile([P, CODES], F32)
-        for a in range(CODE_TILES):
-            nc.tensor.matmul(
-                out=spread[:, a * P : (a + 1) * P],
-                lhsT=c_part[:, a : a + 1].to_broadcast([P, P]),
-                rhs=identity[:],
-                start=True,
-                stop=True,
-            )
-        c_term = keep.tile([P, CODES], F32)
-        nc.scalar.activation(out=c_term[:], in_=spread[:], func=FUNC.Identity, bias=2.0, scale=1.0)
-
+        scratch = keep.tile([P, 1 + CHUNKS, PAIR, LENGTH], BF16)
+        c_part_a = keep.tile([P, 1], F32)
+        c_part_b = keep.tile([P, 1], F32)
         o_term = keep.tile([P, ROW_TILES], F32)
-        for chunk in range(CHUNKS):
-            x_rows = x_chunks[chunk]
+        c_term = keep.tile([P, CODES], F32)
+
+        grouped = keep.tile([P, 1 + CHUNKS, PAIR * P * 4], BF16, align_bytes=64)
+        codes = keep.tile([P, 1 + CHUNKS, PAIR * P], U32, align_bytes=64)
+        scales = keep.tile([P, 1 + CHUNKS, PAIR * P], U8, align_bytes=64)
+        both_terms = keep.tile([P, CHUNKS, PAIR * CODES], F32)
+
+        def sums(i):
+            if i == 0:
+                sum_rows_scalar(nc, y_rows[:, 0, :], scratch[:, 0, 0, :], c_part_a[:])
+                sum_rows_vector(nc, y_rows[:, 1, :], scratch[:, 0, 1, :], c_part_b[:])
+            else:
+                for j in range(PAIR):
+                    r = (i - 1) * PAIR + j
+                    sum_rows_vector(nc, pairs[i][:, j, :], scratch[:, i, j, :], o_term[:, r : r + 1])
+
+        def transpose(i):
+            words = pairs[i][:].bitcast(F32)
+            bank = t_psum.tile([P, PAIR, 2, P], F32)
             for j in range(PAIR):
-                r = chunk * PAIR + j
-                sum_rows(nc, x_rows[:, j, :], scratch[:, CODE_TILES + r, :], o_term[:, r : r + 1])
+                for u in range(2):
+                    nc.tensor.transpose(bank[:, j, u, :], words[:, j, u * P : (u + 1) * P], identity[:])
+            nc.scalar.copy(
+                out=grouped[:, i, :].bitcast(F32).rearrange("p (j n u) -> p j n u", j=PAIR, u=2),
+                in_=bank[:].rearrange("p j u n -> p j n u"),
+            )
 
-            x_bank = t_psum.tile([P, PAIR, 2, P], F32, tag="bank")
-            transpose_pair(nc, x_bank, x_rows[:], identity[:])
-            x_grouped = work.tile([P, PAIR * P * 4], BF16, align_bytes=64)
-            x_codes = work.tile([P, PAIR * P], U32, align_bytes=64)
-            x_scales = work.tile([P, PAIR * P], U8, align_bytes=64)
-            quantise_pair(nc, x_bank, x_grouped[:], x_codes[:], x_scales[:])
+        def quantise(i):
+            nc.vector.quantize_mx(
+                out=codes[:, i, :].bitcast(FP8X4), scales=scales[:, i, :], in_=grouped[:, i, :]
+            )
 
-            both_terms = work.tile([P, PAIR * CODES], F32)
-            dot = dot_psum.tile([P, PAIR * CODES], F32)
+        def spread_c_term():
+            spread = c_psum.tile([P, CODES], F32)
+            nc.tensor.transpose(spread[:, 0:P], c_part_a[:].to_broadcast([P, P]), identity[:])
+            nc.tensor.transpose(spread[:, P:CODES], c_part_b[:].to_broadcast([P, P]), identity[:])
+            nc.scalar.activation(out=c_term[:], in_=spread[:], func=FUNC.Identity, bias=2.0, scale=1.0)
+
+        def add_terms(chunk):
             for j in range(PAIR):
                 r = chunk * PAIR + j
                 nc.scalar.activation(
-                    out=both_terms[:, j * CODES : (j + 1) * CODES],
+                    out=both_terms[:, chunk, j * CODES : (j + 1) * CODES],
                     in_=c_term[:],
                     func=FUNC.Identity,
                     bias=o_term[:, r : r + 1],
                     scale=1.0,
                 )
+
+        for i in range(1 + CHUNKS + 1):
+            if i <= CHUNKS:
+                sums(i)
+                transpose(i)
+            if i >= 1:
+                quantise(i - 1)
+        spread_c_term()
+
+        for chunk in range(CHUNKS):
+            add_terms(chunk)
+            dot = dot_psum.tile([P, PAIR * CODES], F32)
+            for j in range(PAIR):
                 nc.tensor.matmul_mx(
                     out=dot[:, j * CODES : (j + 1) * CODES],
-                    lhsT=x_codes[:, j * P : (j + 1) * P].bitcast(FP8X4),
-                    lhsT_scale=x_scales[:, j * P : (j + 1) * P],
-                    rhs=y_codes[:].bitcast(FP8X4),
-                    rhs_scale=y_scales[:],
+                    lhsT=codes[:, 1 + chunk, j * P : (j + 1) * P].bitcast(FP8X4),
+                    lhsT_scale=scales[:, 1 + chunk, j * P : (j + 1) * P],
+                    rhs=codes[:, 0, :].bitcast(FP8X4),
+                    rhs_scale=scales[:, 0, :],
                     start=True,
                     stop=True,
                 )
-
             result = work.tile([P, PAIR * CODES], F32)
             nc.vector.scalar_tensor_tensor(
                 out=result[:],
                 in0=dot[:],
                 scalar=2.0 / CODES,
-                in1=both_terms[:],
+                in1=both_terms[:, chunk, :],
                 op0=ALU.mult,
                 op1=ALU.add,
             )

@@ -143,16 +143,21 @@ def tile_codingclassifier_s_kernel(tc, output, code_book, out):
                     start=True,
                     stop=True,
                 )
-            result = work.tile([P, PAIR * CODES], F32)
-            nc.vector.scalar_tensor_tensor(
-                out=result[:],
-                in0=dot[:],
-                scalar=2.0 / CODES,
-                in1=both_terms[:, chunk, :],
-                op0=ALU.mult,
-                op1=ALU.add,
-            )
-            nc.sync.dma_start(
-                out=out_view[:, chunk * PAIR : (chunk + 1) * PAIR, :],
-                in_=result[:].rearrange("p (j k) -> p j k", j=PAIR),
-            )
+            pieces = PAIR if chunk == CHUNKS - 1 else 1
+            tiles = PAIR // pieces
+            for piece in range(pieces):
+                first = chunk * PAIR + piece * tiles
+                columns = slice(piece * tiles * CODES, (piece + 1) * tiles * CODES)
+                result = work.tile([P, PAIR * CODES], F32, bufs=CHUNKS + 1)
+                nc.vector.scalar_tensor_tensor(
+                    out=result[:, 0 : tiles * CODES],
+                    in0=dot[:, columns],
+                    scalar=2.0 / CODES,
+                    in1=both_terms[:, chunk, columns],
+                    op0=ALU.mult,
+                    op1=ALU.add,
+                )
+                nc.sync.dma_start(
+                    out=out_view[:, first : first + tiles, :],
+                    in_=result[:, 0 : tiles * CODES].rearrange("p (j k) -> p j k", j=tiles),
+                )

from contextlib import ExitStack

import concourse.mybir as mybir
from concourse.masks import make_identity

F32 = mybir.dt.float32
BF16 = mybir.dt.bfloat16
U32 = mybir.dt.uint32
U8 = mybir.dt.uint8
FP8X4 = mybir.dt.float8_e4m3fn_x4
ALU = mybir.AluOpType
FUNC = mybir.ActivationFunctionType

P = 128
ROWS = 1024
CODES = 256
LENGTH = 512
WORDS = LENGTH // 2
ROW_TILES = ROWS // P
CODE_TILES = CODES // P
PAIR = 2
CHUNKS = ROW_TILES // PAIR

FLOPS = 2 * ROWS * CODES * LENGTH


def sum_rows_vector(nc, rows, scratch, total):
    nc.vector.tensor_scalar(
        out=scratch,
        in0=rows,
        scalar1=-1.0 / CODES,
        scalar2=None,
        op0=ALU.mult,
        op1=ALU.add,
        accum_out=total,
    )


def sum_rows_scalar(nc, rows, scratch, total):
    nc.scalar.activation(out=scratch, in_=rows, func=FUNC.Identity, scale=-1.0 / CODES, accum_out=total)


def tile_codingclassifier_s_kernel(tc, output, code_book, out):
    nc = tc.nc
    x_view = output.rearrange("(p r) c -> p r c", r=ROW_TILES)
    out_view = out.rearrange("(p r) k -> p r k", r=ROW_TILES)

    with ExitStack() as ctx:
        ctx.enter_context(tc.manual_schedule())
        keep = ctx.enter_context(tc.tile_pool(name="keep", bufs=1))
        work = ctx.enter_context(tc.tile_pool(name="work", bufs=CHUNKS))
        t_psum = ctx.enter_context(tc.psum_pool(name="t_psum", bufs=4))
        dot_psum = ctx.enter_context(tc.psum_pool(name="dot_psum", bufs=3))
        c_psum = ctx.enter_context(tc.psum_pool(name="c_psum", bufs=1))

        y_rows = keep.tile([P, PAIR, LENGTH], BF16)
        nc.sync.dma_start(out=y_rows[:], in_=code_book.rearrange("(a p) c -> p a c", p=P))
        pairs = [y_rows]
        for chunk in range(CHUNKS):
            x_rows = work.tile([P, PAIR, LENGTH], BF16)
            nc.sync.dma_start(out=x_rows[:], in_=x_view[:, chunk * PAIR : (chunk + 1) * PAIR, :])
            pairs.append(x_rows)

        identity = keep.tile([P, P], F32)
        make_identity(nc, identity[:])

        warm = keep.tile([P, 1], F32)
        nc.vector.memset(warm[:], 0.0)
        warmed = keep.tile([P, 1], F32)
        nc.scalar.activation(out=warmed[:], in_=warm[:], func=FUNC.Identity)

        scratch = keep.tile([P, 1 + CHUNKS, PAIR, LENGTH], BF16)
        c_part_a = keep.tile([P, 1], F32)
        c_part_b = keep.tile([P, 1], F32)
        o_term = keep.tile([P, ROW_TILES], F32)
        c_term = keep.tile([P, CODES], F32)

        grouped = keep.tile([P, 1 + CHUNKS, PAIR * P * 4], BF16, align_bytes=64)
        codes = keep.tile([P, 1 + CHUNKS, PAIR * P], U32, align_bytes=64)
        scales = keep.tile([P, 1 + CHUNKS, PAIR * P], U8, align_bytes=64)
        both_terms = keep.tile([P, CHUNKS, PAIR * CODES], F32)

        def sums(i):
            if i == 0:
                sum_rows_scalar(nc, y_rows[:, 0, :], scratch[:, 0, 0, :], c_part_a[:])
                sum_rows_vector(nc, y_rows[:, 1, :], scratch[:, 0, 1, :], c_part_b[:])
            else:
                for j in range(PAIR):
                    r = (i - 1) * PAIR + j
                    sum_rows_vector(nc, pairs[i][:, j, :], scratch[:, i, j, :], o_term[:, r : r + 1])

        def transpose(i):
            words = pairs[i][:].bitcast(F32)
            bank = t_psum.tile([P, PAIR, 2, P], F32)
            for j in range(PAIR):
                for u in range(2):
                    nc.tensor.transpose(bank[:, j, u, :], words[:, j, u * P : (u + 1) * P], identity[:])
            nc.scalar.copy(
                out=grouped[:, i, :].bitcast(F32).rearrange("p (j n u) -> p j n u", j=PAIR, u=2),
                in_=bank[:].rearrange("p j u n -> p j n u"),
            )

        def quantise(i):
            nc.vector.quantize_mx(
                out=codes[:, i, :].bitcast(FP8X4), scales=scales[:, i, :], in_=grouped[:, i, :]
            )

        def spread_c_term():
            spread = c_psum.tile([P, CODES], F32)
            nc.tensor.transpose(spread[:, 0:P], c_part_a[:].to_broadcast([P, P]), identity[:])
            nc.tensor.transpose(spread[:, P:CODES], c_part_b[:].to_broadcast([P, P]), identity[:])
            nc.scalar.activation(out=c_term[:], in_=spread[:], func=FUNC.Identity, bias=2.0, scale=1.0)

        def add_terms(chunk):
            for j in range(PAIR):
                r = chunk * PAIR + j
                nc.scalar.activation(
                    out=both_terms[:, chunk, j * CODES : (j + 1) * CODES],
                    in_=c_term[:],
                    func=FUNC.Identity,
                    bias=o_term[:, r : r + 1],
                    scale=1.0,
                )

        for i in range(1 + CHUNKS + 1):
            if i <= CHUNKS:
                sums(i)
                transpose(i)
            if i >= 1:
                quantise(i - 1)
        spread_c_term()

        for chunk in range(CHUNKS):
            add_terms(chunk)
            dot = dot_psum.tile([P, PAIR * CODES], F32)
            for j in range(PAIR):
                nc.tensor.matmul_mx(
                    out=dot[:, j * CODES : (j + 1) * CODES],
                    lhsT=codes[:, 1 + chunk, j * P : (j + 1) * P].bitcast(FP8X4),
                    lhsT_scale=scales[:, 1 + chunk, j * P : (j + 1) * P],
                    rhs=codes[:, 0, :].bitcast(FP8X4),
                    rhs_scale=scales[:, 0, :],
                    start=True,
                    stop=True,
                )
            pieces = PAIR if chunk == CHUNKS - 1 else 1
            tiles = PAIR // pieces
            for piece in range(pieces):
                first = chunk * PAIR + piece * tiles
                columns = slice(piece * tiles * CODES, (piece + 1) * tiles * CODES)
                result = work.tile([P, PAIR * CODES], F32, bufs=CHUNKS + 1)
                nc.vector.scalar_tensor_tensor(
                    out=result[:, 0 : tiles * CODES],
                    in0=dot[:, columns],
                    scalar=2.0 / CODES,
                    in1=both_terms[:, chunk, columns],
                    op0=ALU.mult,
                    op1=ALU.add,
                )
                nc.sync.dma_start(
                    out=out_view[:, first : first + tiles, :],
                    in_=result[:, 0 : tiles * CODES].rearrange("p (j k) -> p j k", j=tiles),
                )
